import numpy as np
import ml_dtypes


def mxq(x, axis, fmt="e4m3"):
    dtype, down = {"e4m3": (ml_dtypes.float8_e4m3fn, 7), "e5m2": (ml_dtypes.float8_e5m2, 14)}[fmt]
    v = np.moveaxis(np.asarray(x, np.float32).astype(ml_dtypes.bfloat16).astype(np.float64), axis, -1)
    blocks = v.reshape(v.shape[:-1] + (-1, 32))
    amax = np.abs(blocks).max(-1, keepdims=True)
    byte = np.maximum(np.where(amax > 0, np.frexp(amax)[1] - 1 + 127, 0) - down, 1)
    scale = np.exp2(byte - 127.0)
    codes = (blocks / scale).astype(np.float32).astype(dtype).astype(np.float64)
    return np.moveaxis((codes * scale).reshape(v.shape), -1, axis)


WIDE = False


def mx_kscale(k):
    if not WIDE:
        return np.ones(k)
    levels = np.array([10, -10, 5, -5, 0])
    a = np.random.permutation(np.resize(levels, k // 512 * 4)).reshape(k // 512, 4)
    idx = np.arange(k)
    return np.exp2(a[idx // 512, idx % 128 // 32])


BF16 = ml_dtypes.bfloat16


def bf(x):
    return np.asarray(x, np.float32).astype(BF16)


def f64(x):
    return np.asarray(x).astype(np.float64)


E2M1 = np.array([0.0, 0.5, 1.0, 1.5, 2.0, 3.0, 4.0, 6.0, -0.0, -0.5, -1.0, -1.5, -2.0, -3.0, -4.0, -6.0])


def pack_weight(w, fmt):
    k, n = w.shape
    w = f64(bf(w)).reshape(k // 32, 32, n)
    amax = np.abs(w).max(1)
    if fmt == "e4m3":
        byte = np.frexp(amax)[1] - 1 + 127 - 7
    else:
        mant, ex = np.frexp(amax / 6.0)
        byte = np.where(mant > 0.5, ex, ex - 1) + 127
    byte = np.clip(np.where(amax > 0, byte, 1), 1, 254)
    scaled = (w * np.exp2(127.0 - byte)[:, None, :]).reshape(k, n).astype(np.float32)
    by_word = np.ascontiguousarray(scaled.reshape(k // 512, 128, 4, n).transpose(0, 1, 3, 2))
    if fmt == "e4m3":
        words = by_word.astype(ml_dtypes.float8_e4m3fn).view(np.uint8)
    else:
        c = by_word.astype(ml_dtypes.float4_e2m1fn).view(np.uint8) & 0xF
        words = c[..., 0::2] | (c[..., 1::2] << 4)
    return np.ascontiguousarray(words), np.ascontiguousarray(byte.astype(np.uint8).reshape(k // 512, 16, n))


def unpack_weight(words, scales, fmt):
    g, p, n, _ = words.shape
    if fmt == "e4m3":
        vals = np.ascontiguousarray(words).view(ml_dtypes.float8_e4m3fn).astype(np.float64)
    else:
        nib = np.empty((g, p, n, 4), np.uint8)
        nib[..., 0::2] = words & 0xF
        nib[..., 1::2] = words >> 4
        vals = E2M1[nib]
    vals = vals * np.repeat(np.exp2(scales.astype(np.float64) - 127.0), 8, axis=1)[..., None]
    return vals.transpose(0, 1, 3, 2).reshape(g * 512, n)


N, FIN, FD, F1, F2, F3, E = 1536, 2048, 1024, 512, 256, 128, 2


def elu(v):
    return np.where(v > 0.0, v, np.exp(np.minimum(v, 0.0)) - 1.0)


def setup_inputs():
    s = mx_kscale(FD)
    k = mx_kscale(N)
    t = np.where(np.arange(E) % 2 == 0, k.max(), k.min())
    x = bf(elu(np.random.standard_normal((N, FD))) * s)
    adjacency_matrix = bf(np.random.uniform(size=(E, N, N)) * 0.5 / np.sqrt(N) / t[:, None, None])
    W1 = bf(np.random.standard_normal((E, FD, F1)) / np.sqrt(FD) / s[:, None] * t[:, None, None])
    b1 = bf(np.random.standard_normal(F1) * 0.3)
    Wr1_words, Wr1_scales = pack_weight(np.random.standard_normal((FD, F1)) * 0.3 / np.sqrt(FD) / s[:, None], "e4m3")
    return {
        "x": x,
        "adjacency_matrix": adjacency_matrix,
        "W1": W1,
        "b1": b1,
        "Wr1_words": Wr1_words,
        "Wr1_scales": Wr1_scales,
    }


def reference(x, adjacency_matrix, W1, b1, Wr1_words, Wr1_scales):
    xq = mxq(f64(x), 1, "e4m3")
    support = xq @ mxq(f64(W1), 1, "e4m3")
    agg = (mxq(f64(adjacency_matrix), 2, "e4m3") @ mxq(support, 1, "e4m3")).sum(0)
    return agg + f64(b1) + (xq @ unpack_weight(Wr1_words, Wr1_scales, "e4m3"))

@@ -1,0 +1,229 @@
+import concourse.mybir as mybir
+from concourse.masks import make_identity
+
+BF16 = mybir.dt.bfloat16
+F32 = mybir.dt.float32
+I32 = mybir.dt.int32
+U32 = mybir.dt.uint32
+U8 = mybir.dt.uint8
+FP8X4 = mybir.dt.float8_e4m3fn_x4
+
+P = 128
+PACK = 4
+K_PASS = P * PACK
+BANK = 512
+
+NODES, FEATS, OUT_F, EDGES = 1536, 1024, 512, 2
+BLOCKS = NODES // (2 * P)
+NODE_PASSES = NODES // K_PASS
+FEAT_PASSES = FEATS // K_PASS
+QUARTERS = OUT_F // P
+A_AHEAD = 4
+
+FLOPS = 2 * (EDGES * NODES * FEATS * OUT_F + EDGES * NODES * NODES * OUT_F + NODES * FEATS * OUT_F)
+
+
+def tile_fgg_pa_kernel(tc, x, adjacency_matrix, W1, b1, Wr1_words, Wr1_scales, out):
+    nc = tc.nc
+
+    x_blocks = x.rearrange("(h p r) k -> h p r k", p=P, r=2)
+    a_blocks = adjacency_matrix.rearrange("e (h p r) m -> e h p r m", p=P, r=2)
+    w1_passes = W1.rearrange("e (g p t) f -> e g p t f", p=P, t=PACK)
+    out_tiles = out.rearrange("(h p r) f -> h r p f", p=P, r=2)
+
+    with (
+        tc.tile_pool(name="keep", bufs=1) as keep,
+        tc.tile_pool(name="a_in", bufs=EDGES * A_AHEAD) as a_in,
+        tc.tile_pool(name="stage_w", bufs=1) as stage_w,
+        tc.tile_pool(name="stage_x", bufs=3) as stage_x,
+        tc.tile_pool(name="stage_s", bufs=2) as stage_s,
+        tc.tile_pool(name="stage_a", bufs=4) as stage_a,
+        tc.tile_pool(name="a_mx", bufs=3) as a_mx,
+        tc.tile_pool(name="stage_o", bufs=4) as stage_o,
+        tc.psum_pool(name="psum", bufs=8) as psum,
+        tc.manual_schedule(),
+    ):
+        ident = keep.tile([P, P], F32)
+        bias = keep.tile([P, OUT_F], BF16)
+        x_rows = keep.tile([P, BLOCKS, 2, FEATS], BF16)
+        w1_rows = keep.tile([P, EDGES, FEAT_PASSES, PACK, OUT_F], BF16)
+
+        x_codes = keep.tile([P, BLOCKS, FEAT_PASSES, 2 * P], U32, align_bytes=64)
+        x_scales = keep.tile([P, BLOCKS, FEAT_PASSES, 2 * P], U8, align_bytes=64)
+        w1_codes = keep.tile([P, EDGES, FEAT_PASSES, OUT_F], U32, align_bytes=64)
+        w1_scales = keep.tile([P, EDGES, FEAT_PASSES, OUT_F], U8, align_bytes=64)
+        wr_codes = keep.tile([P, FEAT_PASSES, OUT_F], U32, align_bytes=64)
+        wr_scales = keep.tile([P, FEAT_PASSES, OUT_F], U8, align_bytes=64)
+        s_codes = keep.tile([P, EDGES, NODE_PASSES, OUT_F], U32, align_bytes=64)
+        s_scales = keep.tile([P, EDGES, NODE_PASSES, OUT_F], U8, align_bytes=64)
+
+        a_rows = {}
+        a_quantised = {}
+
+        def load_x(h):
+            nc.sync.dma_start(out=x_rows[:, h], in_=x_blocks[h])
+
+        def load_w1(e):
+            for g in range(FEAT_PASSES):
+                nc.sync.dma_start(out=w1_rows[:, e, g], in_=w1_passes[e, g])
+
+        def load_wr1():
+            for g in range(FEAT_PASSES):
+                nc.sync.dma_start(
+                    out=wr_codes[:, g].bitcast(I32),
+                    in_=Wr1_words[g].rearrange("p n t -> p (n t)").bitcast(I32),
+                )
+            for quad in range(4):
+                nc.sync.dma_start(
+                    out=wr_scales[32 * quad : 32 * quad + 4].bitcast(I32),
+                    in_=Wr1_scales[:, 4 * quad : 4 * quad + 4, :].rearrange("g s n -> s g n").bitcast(I32),
+                )
+
+        def load_a(h):
+            for e in range(EDGES):
+                rows = a_in.tile([P, 2, NODES], BF16)
+                nc.sync.dma_start(out=rows[:], in_=a_blocks[e, h])
+                a_rows[(e, h)] = rows
+
+        def quantise_w1(e):
+            w1_grouped = stage_w.tile([P, FEAT_PASSES, OUT_F, PACK], BF16, align_bytes=64)
+            for g in range(FEAT_PASSES):
+                nc.vector.tensor_copy(
+                    out=w1_grouped[:, g].rearrange("p (c i) t -> p c t i", i=4),
+                    in_=w1_rows[:, e, g].rearrange("p t (c i) -> p c t i", i=4),
+                )
+            for g in range(FEAT_PASSES):
+                nc.vector.quantize_mx(
+                    out=w1_codes[:, e, g].bitcast(FP8X4),
+                    scales=w1_scales[:, e, g],
+                    in_=w1_grouped[:, g].rearrange("p f t -> p (f t)"),
+                )
+
+        def transpose_words(bank, rows, first_word, step):
+            for u in range(2):
+                for r in range(2):
+                    words = rows[:, r].bitcast(F32)
+                    start = first_word(u)
+                    nc.tensor.transpose(
+                        bank[:, (2 * u + r) * P : (2 * u + r + 1) * P],
+                        words[:, start : start + step * (P - 1) + 1 : step],
+                        ident[:],
+                    )
+
+        def empty_words(grouped, bank):
+            nc.scalar.copy(
+                out=grouped.bitcast(F32).rearrange("p (n u) -> p n u", u=2),
+                in_=bank[:].rearrange("p (u n) -> p n u", u=2),
+            )
+
+        def transpose_x(h):
+            x_grouped = stage_x.tile([P, FEAT_PASSES, PACK * 2 * P], BF16, align_bytes=64)
+            for g in range(FEAT_PASSES):
+                bank = psum.tile([P, BANK], F32, tag="bank")
+                transpose_words(bank, x_rows[:, h], lambda u: 2 * P * g + u, 2)
+                empty_words(x_grouped[:, g], bank)
+            nc.vector.quantize_mx(
+                out=x_codes[:, h].rearrange("p g n -> p (g n)").bitcast(FP8X4),
+                scales=x_scales[:, h].rearrange("p g n -> p (g n)"),
+                in_=x_grouped[:].rearrange("p g n -> p (g n)"),
+            )
+
+        def stage1(c, e):
+            s_grouped = stage_s.tile([P, OUT_F, PACK], BF16, align_bytes=64)
+            for q in range(QUARTERS):
+                f_cols = slice(q * P, (q + 1) * P)
+                bank = psum.tile([P, BANK], F32, tag="bank")
+                for t in range(PACK):
+                    h, r = 2 * c + t // 2, t % 2
+                    n_cols = slice(r * P, (r + 1) * P)
+                    for g in range(FEAT_PASSES):
+                        nc.tensor.matmul_mx(
+                            out=bank[:, t * P : (t + 1) * P],
+                            lhsT=x_codes[:, h, g, n_cols].bitcast(FP8X4),
+                            lhsT_scale=x_scales[:, h, g, n_cols],
+                            rhs=w1_codes[:, e, g, f_cols].bitcast(FP8X4),
+                            rhs_scale=w1_scales[:, e, g, f_cols],
+                            start=(g == 0),
+                            stop=(g == FEAT_PASSES - 1),
+                        )
+                copy_out = nc.vector.tensor_copy if q == 0 else nc.scalar.copy
+                copy_out(out=s_grouped[:, f_cols, :], in_=bank[:].rearrange("p (t f) -> p f t", t=PACK))
+            nc.vector.quantize_mx(
+                out=s_codes[:, e, c].bitcast(FP8X4),
+                scales=s_scales[:, e, c],
+                in_=s_grouped[:].rearrange("p f t -> p (f t)"),
+            )
+
+        def transpose_a(h):
+            a_codes = a_mx.tile([P, NODE_PASSES, EDGES, 2 * P], U32, align_bytes=64)
+            a_scales = a_mx.tile([P, NODE_PASSES, EDGES, 2 * P], U8, align_bytes=64)
+            for c in range(NODE_PASSES):
+                a_grouped = stage_a.tile([P, EDGES, PACK * 2 * P], BF16, align_bytes=64)
+                for e in range(EDGES):
+                    bank = psum.tile([P, BANK], F32, tag="bank")
+                    transpose_words(bank, a_rows[(e, h)], lambda u: 2 * P * c + P * u, 1)
+                    empty_words(a_grouped[:, e], bank)
+                nc.vector.quantize_mx(
+                    out=a_codes[:, c].rearrange("p e n -> p (e n)").bitcast(FP8X4),
+                    scales=a_scales[:, c].rearrange("p e n -> p (e n)"),
+                    in_=a_grouped[:].rearrange("p e n -> p (e n)"),
+                )
+            a_quantised[h] = (a_codes, a_scales)
+            if h + A_AHEAD < BLOCKS:
+                load_a(h + A_AHEAD)
+
+        def stage2(h):
+            a_codes, a_scales = a_quantised[h]
+            for r in range(2):
+                n_cols = slice(r * P, (r + 1) * P)
+                bank = psum.tile([P, BANK], F32, tag="bank")
+                for g in range(FEAT_PASSES):
+                    nc.tensor.matmul_mx(
+                        out=bank[:],
+                        lhsT=x_codes[:, h, g, n_cols].bitcast(FP8X4),
+                        lhsT_scale=x_scales[:, h, g, n_cols],
+                        rhs=wr_codes[:, g].bitcast(FP8X4),
+                        rhs_scale=wr_scales[:, g],
+                        start=(g == 0),
+                        stop=False,
+                    )
+                for c in range(NODE_PASSES):
+                    for e in range(EDGES):
+                        nc.tensor.matmul_mx(
+                            out=bank[:],
+                            lhsT=a_codes[:, c, e, n_cols].bitcast(FP8X4),
+                            lhsT_scale=a_scales[:, c, e, n_cols],
+                            rhs=s_codes[:, e, c].bitcast(FP8X4),
+                            rhs_scale=s_scales[:, e, c],
+                            start=False,
+                            stop=(c == NODE_PASSES - 1 and e == EDGES - 1),
+                        )
+                out_rows = stage_o.tile([P, OUT_F], F32)
+                nc.vector.tensor_tensor(out=out_rows[:], in0=bank[:], in1=bias[:], op=mybir.AluOpType.add)
+                nc.sync.dma_start(out=out_tiles[h, r], in_=out_rows[:])
+
+        make_identity(nc, ident[:])
+        nc.vector.memset(wr_scales[:].rearrange("p g n -> p (g n)").bitcast(I32), 0)
+
+        load_w1(0)
+        for h in range(BLOCKS):
+            load_x(h)
+        load_w1(1)
+        load_wr1()
+        for h in range(A_AHEAD):
+            load_a(h)
+        nc.sync.dma_start(out=bias[:], in_=b1.partition_broadcast(P))
+
+        quantise_w1(0)
+        for h in range(BLOCKS):
+            transpose_x(h)
+        quantise_w1(1)
+        for e in range(EDGES):
+            for c in range(NODE_PASSES):
+                stage1(c, e)
+
+        transpose_a(0)
+        for h in range(BLOCKS):
+            if h + 1 < BLOCKS:
+                transpose_a(h + 1)
+            stage2(h)

@@ -176,31 +176,37 @@ def tile_fgg_pa_kernel(tc, x, adjacency_matrix, W1, b1, Wr1_words, Wr1_scales, o
             a_codes, a_scales = a_quantised[h]
             for r in range(2):
                 n_cols = slice(r * P, (r + 1) * P)
-                bank = psum.tile([P, BANK], F32, tag="bank")
-                for g in range(FEAT_PASSES):
-                    nc.tensor.matmul_mx(
-                        out=bank[:],
-                        lhsT=x_codes[:, h, g, n_cols].bitcast(FP8X4),
-                        lhsT_scale=x_scales[:, h, g, n_cols],
-                        rhs=wr_codes[:, g].bitcast(FP8X4),
-                        rhs_scale=wr_scales[:, g],
-                        start=(g == 0),
-                        stop=False,
-                    )
-                for c in range(NODE_PASSES):
-                    for e in range(EDGES):
+                parts = 2 if (h == BLOCKS - 1 and r == 1) else 1
+                width = OUT_F // parts
+                for part in range(parts):
+                    f_cols = slice(part * width, (part + 1) * width)
+                    bank = psum.tile([P, BANK], F32, tag="bank")
+                    for g in range(FEAT_PASSES):
                         nc.tensor.matmul_mx(
-                            out=bank[:],
-                            lhsT=a_codes[:, c, e, n_cols].bitcast(FP8X4),
-                            lhsT_scale=a_scales[:, c, e, n_cols],
-                            rhs=s_codes[:, e, c].bitcast(FP8X4),
-                            rhs_scale=s_scales[:, e, c],
-                            start=False,
-                            stop=(c == NODE_PASSES - 1 and e == EDGES - 1),
+                            out=bank[:, :width],
+                            lhsT=x_codes[:, h, g, n_cols].bitcast(FP8X4),
+                            lhsT_scale=x_scales[:, h, g, n_cols],
+                            rhs=wr_codes[:, g, f_cols].bitcast(FP8X4),
+                            rhs_scale=wr_scales[:, g, f_cols],
+                            start=(g == 0),
+                            stop=False,
                         )
-                out_rows = stage_o.tile([P, OUT_F], F32)
-                nc.vector.tensor_tensor(out=out_rows[:], in0=bank[:], in1=bias[:], op=mybir.AluOpType.add)
-                nc.sync.dma_start(out=out_tiles[h, r], in_=out_rows[:])
+                    for c in range(NODE_PASSES):
+                        for e in range(EDGES):
+                            nc.tensor.matmul_mx(
+                                out=bank[:, :width],
+                                lhsT=a_codes[:, c, e, n_cols].bitcast(FP8X4),
+                                lhsT_scale=a_scales[:, c, e, n_cols],
+                                rhs=s_codes[:, e, c, f_cols].bitcast(FP8X4),
+                                rhs_scale=s_scales[:, e, c, f_cols],
+                                start=False,
+                                stop=(c == NODE_PASSES - 1 and e == EDGES - 1),
+                            )
+                    out_rows = stage_o.tile([P, OUT_F], F32)
+                    nc.vector.tensor_tensor(
+                        out=out_rows[:, :width], in0=bank[:, :width], in1=bias[:, f_cols], op=mybir.AluOpType.add
+                    )
+                    nc.sync.dma_start(out=out_tiles[h, r][:, f_cols], in_=out_rows[:, :width])
 
         make_identity(nc, ident[:])
         nc.vector.memset(wr_scales[:].rearrange("p g n -> p (g n)").bitcast(I32), 0)
@@ -218,11 +224,13 @@ def tile_fgg_pa_kernel(tc, x, adjacency_matrix, W1, b1, Wr1_words, Wr1_scales, o
         for h in range(BLOCKS):
             transpose_x(h)
         quantise_w1(1)
-        for e in range(EDGES):
-            for c in range(NODE_PASSES):
-                stage1(c, e)
-
+        for c in range(NODE_PASSES):
+            stage1(c, 0)
+        stage1(0, 1)
+        stage1(1, 1)
         transpose_a(0)
+        stage1(2, 1)
+
         for h in range(BLOCKS):
             if h + 1 < BLOCKS:
                 transpose_a(h + 1)

import concourse.mybir as mybir
from concourse.masks import make_identity

BF16 = mybir.dt.bfloat16
F32 = mybir.dt.float32
I32 = mybir.dt.int32
U32 = mybir.dt.uint32
U8 = mybir.dt.uint8
FP8X4 = mybir.dt.float8_e4m3fn_x4

P = 128
PACK = 4
K_PASS = P * PACK
BANK = 512

NODES, FEATS, OUT_F, EDGES = 1536, 1024, 512, 2
BLOCKS = NODES // (2 * P)
NODE_PASSES = NODES // K_PASS
FEAT_PASSES = FEATS // K_PASS
QUARTERS = OUT_F // P
A_AHEAD = 4

FLOPS = 2 * (EDGES * NODES * FEATS * OUT_F + EDGES * NODES * NODES * OUT_F + NODES * FEATS * OUT_F)


def tile_fgg_pa_kernel(tc, x, adjacency_matrix, W1, b1, Wr1_words, Wr1_scales, out):
    nc = tc.nc

    x_blocks = x.rearrange("(h p r) k -> h p r k", p=P, r=2)
    a_blocks = adjacency_matrix.rearrange("e (h p r) m -> e h p r m", p=P, r=2)
    w1_passes = W1.rearrange("e (g p t) f -> e g p t f", p=P, t=PACK)
    out_tiles = out.rearrange("(h p r) f -> h r p f", p=P, r=2)

    with (
        tc.tile_pool(name="keep", bufs=1) as keep,
        tc.tile_pool(name="a_in", bufs=EDGES * A_AHEAD) as a_in,
        tc.tile_pool(name="stage_w", bufs=1) as stage_w,
        tc.tile_pool(name="stage_x", bufs=3) as stage_x,
        tc.tile_pool(name="stage_s", bufs=2) as stage_s,
        tc.tile_pool(name="stage_a", bufs=4) as stage_a,
        tc.tile_pool(name="a_mx", bufs=3) as a_mx,
        tc.tile_pool(name="stage_o", bufs=4) as stage_o,
        tc.psum_pool(name="psum", bufs=8) as psum,
        tc.manual_schedule(),
    ):
        ident = keep.tile([P, P], F32)
        bias = keep.tile([P, OUT_F], BF16)
        x_rows = keep.tile([P, BLOCKS, 2, FEATS], BF16)
        w1_rows = keep.tile([P, EDGES, FEAT_PASSES, PACK, OUT_F], BF16)

        x_codes = keep.tile([P, BLOCKS, FEAT_PASSES, 2 * P], U32, align_bytes=64)
        x_scales = keep.tile([P, BLOCKS, FEAT_PASSES, 2 * P], U8, align_bytes=64)
        w1_codes = keep.tile([P, EDGES, FEAT_PASSES, OUT_F], U32, align_bytes=64)
        w1_scales = keep.tile([P, EDGES, FEAT_PASSES, OUT_F], U8, align_bytes=64)
        wr_codes = keep.tile([P, FEAT_PASSES, OUT_F], U32, align_bytes=64)
        wr_scales = keep.tile([P, FEAT_PASSES, OUT_F], U8, align_bytes=64)
        s_codes = keep.tile([P, EDGES, NODE_PASSES, OUT_F], U32, align_bytes=64)
        s_scales = keep.tile([P, EDGES, NODE_PASSES, OUT_F], U8, align_bytes=64)

        a_rows = {}
        a_quantised = {}

        def load_x(h):
            nc.sync.dma_start(out=x_rows[:, h], in_=x_blocks[h])

        def load_w1(e):
            for g in range(FEAT_PASSES):
                nc.sync.dma_start(out=w1_rows[:, e, g], in_=w1_passes[e, g])

        def load_wr1():
            for g in range(FEAT_PASSES):
                nc.sync.dma_start(
                    out=wr_codes[:, g].bitcast(I32),
                    in_=Wr1_words[g].rearrange("p n t -> p (n t)").bitcast(I32),
                )
            for quad in range(4):
                nc.sync.dma_start(
                    out=wr_scales[32 * quad : 32 * quad + 4].bitcast(I32),
                    in_=Wr1_scales[:, 4 * quad : 4 * quad + 4, :].rearrange("g s n -> s g n").bitcast(I32),
                )

        def load_a(h):
            for e in range(EDGES):
                rows = a_in.tile([P, 2, NODES], BF16)
                nc.sync.dma_start(out=rows[:], in_=a_blocks[e, h])
                a_rows[(e, h)] = rows

        def quantise_w1(e):
            w1_grouped = stage_w.tile([P, FEAT_PASSES, OUT_F, PACK], BF16, align_bytes=64)
            for g in range(FEAT_PASSES):
                nc.vector.tensor_copy(
                    out=w1_grouped[:, g].rearrange("p (c i) t -> p c t i", i=4),
                    in_=w1_rows[:, e, g].rearrange("p t (c i) -> p c t i", i=4),
                )
            for g in range(FEAT_PASSES):
                nc.vector.quantize_mx(
                    out=w1_codes[:, e, g].bitcast(FP8X4),
                    scales=w1_scales[:, e, g],
                    in_=w1_grouped[:, g].rearrange("p f t -> p (f t)"),
                )

        def transpose_words(bank, rows, first_word, step):
            for u in range(2):
                for r in range(2):
                    words = rows[:, r].bitcast(F32)
                    start = first_word(u)
                    nc.tensor.transpose(
                        bank[:, (2 * u + r) * P : (2 * u + r + 1) * P],
                        words[:, start : start + step * (P - 1) + 1 : step],
                        ident[:],
                    )

        def empty_words(grouped, bank):
            nc.scalar.copy(
                out=grouped.bitcast(F32).rearrange("p (n u) -> p n u", u=2),
                in_=bank[:].rearrange("p (u n) -> p n u", u=2),
            )

        def transpose_x(h):
            x_grouped = stage_x.tile([P, FEAT_PASSES, PACK * 2 * P], BF16, align_bytes=64)
            for g in range(FEAT_PASSES):
                bank = psum.tile([P, BANK], F32, tag="bank")
                transpose_words(bank, x_rows[:, h], lambda u: 2 * P * g + u, 2)
                empty_words(x_grouped[:, g], bank)
            nc.vector.quantize_mx(
                out=x_codes[:, h].rearrange("p g n -> p (g n)").bitcast(FP8X4),
                scales=x_scales[:, h].rearrange("p g n -> p (g n)"),
                in_=x_grouped[:].rearrange("p g n -> p (g n)"),
            )

        def stage1(c, e):
            s_grouped = stage_s.tile([P, OUT_F, PACK], BF16, align_bytes=64)
            for q in range(QUARTERS):
                f_cols = slice(q * P, (q + 1) * P)
                bank = psum.tile([P, BANK], F32, tag="bank")
                for t in range(PACK):
                    h, r = 2 * c + t // 2, t % 2
                    n_cols = slice(r * P, (r + 1) * P)
                    for g in range(FEAT_PASSES):
                        nc.tensor.matmul_mx(
                            out=bank[:, t * P : (t + 1) * P],
                            lhsT=x_codes[:, h, g, n_cols].bitcast(FP8X4),
                            lhsT_scale=x_scales[:, h, g, n_cols],
                            rhs=w1_codes[:, e, g, f_cols].bitcast(FP8X4),
                            rhs_scale=w1_scales[:, e, g, f_cols],
                            start=(g == 0),
                            stop=(g == FEAT_PASSES - 1),
                        )
                copy_out = nc.vector.tensor_copy if q == 0 else nc.scalar.copy
                copy_out(out=s_grouped[:, f_cols, :], in_=bank[:].rearrange("p (t f) -> p f t", t=PACK))
            nc.vector.quantize_mx(
                out=s_codes[:, e, c].bitcast(FP8X4),
                scales=s_scales[:, e, c],
                in_=s_grouped[:].rearrange("p f t -> p (f t)"),
            )

        def transpose_a(h):
            a_codes = a_mx.tile([P, NODE_PASSES, EDGES, 2 * P], U32, align_bytes=64)
            a_scales = a_mx.tile([P, NODE_PASSES, EDGES, 2 * P], U8, align_bytes=64)
            for c in range(NODE_PASSES):
                a_grouped = stage_a.tile([P, EDGES, PACK * 2 * P], BF16, align_bytes=64)
                for e in range(EDGES):
                    bank = psum.tile([P, BANK], F32, tag="bank")
                    transpose_words(bank, a_rows[(e, h)], lambda u: 2 * P * c + P * u, 1)
                    empty_words(a_grouped[:, e], bank)
                nc.vector.quantize_mx(
                    out=a_codes[:, c].rearrange("p e n -> p (e n)").bitcast(FP8X4),
                    scales=a_scales[:, c].rearrange("p e n -> p (e n)"),
                    in_=a_grouped[:].rearrange("p e n -> p (e n)"),
                )
            a_quantised[h] = (a_codes, a_scales)
            if h + A_AHEAD < BLOCKS:
                load_a(h + A_AHEAD)

        def stage2(h):
            a_codes, a_scales = a_quantised[h]
            for r in range(2):
                n_cols = slice(r * P, (r + 1) * P)
                parts = 2 if (h == BLOCKS - 1 and r == 1) else 1
                width = OUT_F // parts
                for part in range(parts):
                    f_cols = slice(part * width, (part + 1) * width)
                    bank = psum.tile([P, BANK], F32, tag="bank")
                    for g in range(FEAT_PASSES):
                        nc.tensor.matmul_mx(
                            out=bank[:, :width],
                            lhsT=x_codes[:, h, g, n_cols].bitcast(FP8X4),
                            lhsT_scale=x_scales[:, h, g, n_cols],
                            rhs=wr_codes[:, g, f_cols].bitcast(FP8X4),
                            rhs_scale=wr_scales[:, g, f_cols],
                            start=(g == 0),
                            stop=False,
                        )
                    for c in range(NODE_PASSES):
                        for e in range(EDGES):
                            nc.tensor.matmul_mx(
                                out=bank[:, :width],
                                lhsT=a_codes[:, c, e, n_cols].bitcast(FP8X4),
                                lhsT_scale=a_scales[:, c, e, n_cols],
                                rhs=s_codes[:, e, c, f_cols].bitcast(FP8X4),
                                rhs_scale=s_scales[:, e, c, f_cols],
                                start=False,
                                stop=(c == NODE_PASSES - 1 and e == EDGES - 1),
                            )
                    out_rows = stage_o.tile([P, OUT_F], F32)
                    nc.vector.tensor_tensor(
                        out=out_rows[:, :width], in0=bank[:, :width], in1=bias[:, f_cols], op=mybir.AluOpType.add
                    )
                    nc.sync.dma_start(out=out_tiles[h, r][:, f_cols], in_=out_rows[:, :width])

        make_identity(nc, ident[:])
        nc.vector.memset(wr_scales[:].rearrange("p g n -> p (g n)").bitcast(I32), 0)

        load_w1(0)
        for h in range(BLOCKS):
            load_x(h)
        load_w1(1)
        load_wr1()
        for h in range(A_AHEAD):
            load_a(h)
        nc.sync.dma_start(out=bias[:], in_=b1.partition_broadcast(P))

        quantise_w1(0)
        for h in range(BLOCKS):
            transpose_x(h)
        quantise_w1(1)
        for c in range(NODE_PASSES):
            stage1(c, 0)
        stage1(0, 1)
        stage1(1, 1)
        transpose_a(0)
        stage1(2, 1)

        for h in range(BLOCKS):
            if h + 1 < BLOCKS:
                transpose_a(h + 1)
            stage2(h)
